import numpy as np
import ml_dtypes

BF16 = ml_dtypes.bfloat16


def bf(x):
    return np.asarray(x, np.float32).astype(BF16)


def f32(x):
    return np.asarray(x, np.float32)


def f64(x):
    return np.asarray(x).astype(np.float64)


def striped(idx):
    return np.tile(idx.reshape(-1, 16).T, (8, 1))


S, R, C, T, B, N = 2048, 128, 256, 3, 512, 1536


def setup_inputs():
    return {
        "table": bf(np.random.standard_normal((R, S))),
        "w1": bf(np.random.standard_normal((R, C)) / np.sqrt(R)),
        "b1": f32(0.1 * np.random.standard_normal((C, 1))),
        "w2": bf(np.random.standard_normal((T, C, C)) / np.sqrt(T * C)),
        "b2": f32(0.1 * np.random.standard_normal((C, 1))),
        "wfc1": bf(np.random.standard_normal((C, C)) / np.sqrt(C)),
        "bfc1": f32(0.1 * np.random.standard_normal((C, 1))),
        "offs": striped(np.random.permutation(np.tile(np.arange(S), 2))[:N]),
    }


def reference(table, w1, b1, w2, b2, wfc1, bfc1, offs):
    idx = offs[:16].T.reshape(-1)
    h1 = np.maximum(f64(w1).T @ f64(table)[:, idx] + f64(b1), 0.0)
    acc = sum(f64(w2)[t].T @ h1[:, t * B:(t + 1) * B] for t in range(T))
    h2 = np.maximum(acc + f64(b2), 0.0)
    return np.maximum(f64(wfc1).T @ h2 + f64(bfc1), 0.0)

@@ -1,0 +1,113 @@
+import concourse.mybir as mybir
+
+BF16 = mybir.dt.bfloat16
+F32 = mybir.dt.float32
+U16 = mybir.dt.uint16
+RELU = mybir.ActivationFunctionType.Relu
+ADD = mybir.AluOpType.add
+MAX = mybir.AluOpType.max
+
+P = 128
+S = 2048
+C = 256
+T = 3
+B = 512
+N = T * B
+H = C // P
+WIDTHS = (320, 192)
+STARTS = (0, 320)
+PIECES = 4
+
+FLOPS = 2 * (P * C * N + T * C * C * B + C * C * B)
+
+
+def bias_relu(nc, turn, out, acc, bias):
+    if turn % 2 == 0:
+        nc.vector.tensor_scalar(out, acc, bias, 0.0, ADD, MAX)
+    else:
+        nc.scalar.activation(out, acc, RELU, bias=bias)
+
+
+def tile_costcomodel_kernel(tc, table, w1, b1, w2, b2, wfc1, bfc1, offs, out):
+    nc = tc.nc
+    with (
+        tc.tile_pool(name="held", bufs=1) as held,
+        tc.psum_pool(name="banks", bufs=8) as banks,
+    ):
+        offsets = held.tile([P, N // 16], U16, name="offsets")
+        nc.sync.dma_start(offsets[:], offs)
+        w1_sb = held.tile([P, C], BF16, name="w1_sb")
+        nc.scalar.dma_start(w1_sb[:], w1)
+        table_sb = held.tile([P, S], BF16, name="table_sb")
+        for q in range(PIECES):
+            queue = nc.sync if q % 2 == 0 else nc.scalar
+            piece = slice(q * (S // PIECES), (q + 1) * (S // PIECES))
+            queue.dma_start(table_sb[:, piece], table[:, piece])
+        b1_sb = held.tile([P, H], F32, name="b1_sb")
+        b2_sb = held.tile([P, H], F32, name="b2_sb")
+        bfc1_sb = held.tile([P, H], F32, name="bfc1_sb")
+        w2_sb = held.tile([P, T * H, C], BF16, name="w2_sb")
+        wfc1_sb = held.tile([P, H, C], BF16, name="wfc1_sb")
+        with nc.allow_non_contiguous_dma(reason="a bias of 256 values, one value to a partition"):
+            nc.sync.dma_start(b1_sb[:], b1.rearrange("(h p) one -> p (h one)", p=P))
+            nc.scalar.dma_start(w2_sb[:], w2.rearrange("t (h p) d -> p (t h) d", p=P))
+            nc.sync.dma_start(b2_sb[:], b2.rearrange("(h p) one -> p (h one)", p=P))
+            nc.sync.dma_start(wfc1_sb[:], wfc1.rearrange("(h p) e -> p h e", p=P))
+            nc.sync.dma_start(bfc1_sb[:], bfc1.rearrange("(h p) one -> p (h one)", p=P))
+
+        turn = 0
+
+        h1 = {}
+        for t in range(T):
+            picked = table_sb[:].indirect(offsets[:, t * (B // 16) : (t + 1) * (B // 16)])
+            for h in range(H):
+                proj = banks.tile([P, B], F32, name="bank")
+                nc.tensor.matmul(proj[:], w1_sb[:, h * P : (h + 1) * P], picked, start=True, stop=True)
+                h1[t, h] = held.tile([P, B], BF16, name=f"h1_{t}_{h}")
+                bias_relu(nc, turn, h1[t, h][:], proj[:], b1_sb[:, h : h + 1])
+                turn += 1
+
+        early = (T - 1) * H
+        h2 = {}
+        for c, (lo, wide) in enumerate(zip(STARTS, WIDTHS)):
+            merged = {}
+            for g in range(H):
+                merged[g] = banks.tile([P, wide], F32, name="bank")
+                for k in range(early):
+                    nc.tensor.matmul(
+                        merged[g][:],
+                        w2_sb[:, k, g * P : (g + 1) * P],
+                        h1[k // H, k % H][:, lo : lo + wide],
+                        start=(k == 0),
+                        stop=False,
+                    )
+            for g in range(H):
+                for k in range(early, T * H):
+                    nc.tensor.matmul(
+                        merged[g][:],
+                        w2_sb[:, k, g * P : (g + 1) * P],
+                        h1[k // H, k % H][:, lo : lo + wide],
+                        start=False,
+                        stop=(k == T * H - 1),
+                    )
+                h2[g, c] = held.tile([P, wide], BF16, name=f"h2_{g}_{c}")
+                bias_relu(nc, turn, h2[g, c][:], merged[g][:], b2_sb[:, g : g + 1])
+                turn += 1
+
+        for c, (lo, wide) in enumerate(zip(STARTS, WIDTHS)):
+            for e in range(H):
+                dense = banks.tile([P, wide], F32, name="bank")
+                for g in range(H):
+                    nc.tensor.matmul(
+                        dense[:],
+                        wfc1_sb[:, g, e * P : (e + 1) * P],
+                        h2[g, c][:],
+                        start=(g == 0),
+                        stop=(g == H - 1),
+                    )
+                result = held.tile([P, wide], F32, name=f"result_{e}_{c}")
+                bias_relu(nc, turn, result[:], dense[:], bfc1_sb[:, e : e + 1])
+                last = c == len(WIDTHS) - 1 and e == H - 1
+                queue = nc.scalar if last else nc.sync
+                queue.dma_start(out[e * P : (e + 1) * P, lo : lo + wide], result[:])
+                turn += 1

@@ -16,6 +16,7 @@ N = T * B
 H = C // P
 WIDTHS = (320, 192)
 STARTS = (0, 320)
+LINE = 256
 PIECES = 4
 
 FLOPS = 2 * (P * C * N + T * C * C * B + C * C * B)
@@ -34,11 +35,11 @@ def tile_costcomodel_kernel(tc, table, w1, b1, w2, b2, wfc1, bfc1, offs, out):
         tc.tile_pool(name="held", bufs=1) as held,
         tc.psum_pool(name="banks", bufs=8) as banks,
     ):
-        offsets = held.tile([P, N // 16], U16, name="offsets")
+        offsets = held.tile([P, N // 16], U16, name="offsets", align_bytes=LINE)
         nc.sync.dma_start(offsets[:], offs)
-        w1_sb = held.tile([P, C], BF16, name="w1_sb")
+        w1_sb = held.tile([P, C], BF16, name="w1_sb", align_bytes=LINE)
         nc.scalar.dma_start(w1_sb[:], w1)
-        table_sb = held.tile([P, S], BF16, name="table_sb")
+        table_sb = held.tile([P, S], BF16, name="table_sb", align_bytes=LINE)
         for q in range(PIECES):
             queue = nc.sync if q % 2 == 0 else nc.scalar
             piece = slice(q * (S // PIECES), (q + 1) * (S // PIECES))
@@ -46,8 +47,8 @@ def tile_costcomodel_kernel(tc, table, w1, b1, w2, b2, wfc1, bfc1, offs, out):
         b1_sb = held.tile([P, H], F32, name="b1_sb")
         b2_sb = held.tile([P, H], F32, name="b2_sb")
         bfc1_sb = held.tile([P, H], F32, name="bfc1_sb")
-        w2_sb = held.tile([P, T * H, C], BF16, name="w2_sb")
-        wfc1_sb = held.tile([P, H, C], BF16, name="wfc1_sb")
+        w2_sb = held.tile([P, T * H, C], BF16, name="w2_sb", align_bytes=LINE)
+        wfc1_sb = held.tile([P, H, C], BF16, name="wfc1_sb", align_bytes=LINE)
         with nc.allow_non_contiguous_dma(reason="a bias of 256 values, one value to a partition"):
             nc.sync.dma_start(b1_sb[:], b1.rearrange("(h p) one -> p (h one)", p=P))
             nc.scalar.dma_start(w2_sb[:], w2.rearrange("t (h p) d -> p (t h) d", p=P))
@@ -105,7 +106,7 @@ def tile_costcomodel_kernel(tc, table, w1, b1, w2, b2, wfc1, bfc1, offs, out):
                         start=(g == 0),
                         stop=(g == H - 1),
                     )
-                result = held.tile([P, wide], F32, name=f"result_{e}_{c}")
+                result = held.tile([P, wide], F32, name=f"result_{e}_{c}", align_bytes=LINE)
                 bias_relu(nc, turn, result[:], dense[:], bfc1_sb[:, e : e + 1])
                 last = c == len(WIDTHS) - 1 and e == H - 1
                 queue = nc.scalar if last else nc.sync

import concourse.mybir as mybir

BF16 = mybir.dt.bfloat16
F32 = mybir.dt.float32
U16 = mybir.dt.uint16
RELU = mybir.ActivationFunctionType.Relu
ADD = mybir.AluOpType.add
MAX = mybir.AluOpType.max

P = 128
S = 2048
C = 256
T = 3
B = 512
N = T * B
H = C // P
WIDTHS = (320, 192)
STARTS = (0, 320)
LINE = 256
PIECES = 4

FLOPS = 2 * (P * C * N + T * C * C * B + C * C * B)


def bias_relu(nc, turn, out, acc, bias):
    if turn % 2 == 0:
        nc.vector.tensor_scalar(out, acc, bias, 0.0, ADD, MAX)
    else:
        nc.scalar.activation(out, acc, RELU, bias=bias)


def tile_costcomodel_kernel(tc, table, w1, b1, w2, b2, wfc1, bfc1, offs, out):
    nc = tc.nc
    with (
        tc.tile_pool(name="held", bufs=1) as held,
        tc.psum_pool(name="banks", bufs=8) as banks,
    ):
        offsets = held.tile([P, N // 16], U16, name="offsets", align_bytes=LINE)
        nc.sync.dma_start(offsets[:], offs)
        w1_sb = held.tile([P, C], BF16, name="w1_sb", align_bytes=LINE)
        nc.scalar.dma_start(w1_sb[:], w1)
        table_sb = held.tile([P, S], BF16, name="table_sb", align_bytes=LINE)
        for q in range(PIECES):
            queue = nc.sync if q % 2 == 0 else nc.scalar
            piece = slice(q * (S // PIECES), (q + 1) * (S // PIECES))
            queue.dma_start(table_sb[:, piece], table[:, piece])
        b1_sb = held.tile([P, H], F32, name="b1_sb")
        b2_sb = held.tile([P, H], F32, name="b2_sb")
        bfc1_sb = held.tile([P, H], F32, name="bfc1_sb")
        w2_sb = held.tile([P, T * H, C], BF16, name="w2_sb", align_bytes=LINE)
        wfc1_sb = held.tile([P, H, C], BF16, name="wfc1_sb", align_bytes=LINE)
        with nc.allow_non_contiguous_dma(reason="a bias of 256 values, one value to a partition"):
            nc.sync.dma_start(b1_sb[:], b1.rearrange("(h p) one -> p (h one)", p=P))
            nc.scalar.dma_start(w2_sb[:], w2.rearrange("t (h p) d -> p (t h) d", p=P))
            nc.sync.dma_start(b2_sb[:], b2.rearrange("(h p) one -> p (h one)", p=P))
            nc.sync.dma_start(wfc1_sb[:], wfc1.rearrange("(h p) e -> p h e", p=P))
            nc.sync.dma_start(bfc1_sb[:], bfc1.rearrange("(h p) one -> p (h one)", p=P))

        turn = 0

        h1 = {}
        for t in range(T):
            picked = table_sb[:].indirect(offsets[:, t * (B // 16) : (t + 1) * (B // 16)])
            for h in range(H):
                proj = banks.tile([P, B], F32, name="bank")
                nc.tensor.matmul(proj[:], w1_sb[:, h * P : (h + 1) * P], picked, start=True, stop=True)
                h1[t, h] = held.tile([P, B], BF16, name=f"h1_{t}_{h}")
                bias_relu(nc, turn, h1[t, h][:], proj[:], b1_sb[:, h : h + 1])
                turn += 1

        early = (T - 1) * H
        h2 = {}
        for c, (lo, wide) in enumerate(zip(STARTS, WIDTHS)):
            merged = {}
            for g in range(H):
                merged[g] = banks.tile([P, wide], F32, name="bank")
                for k in range(early):
                    nc.tensor.matmul(
                        merged[g][:],
                        w2_sb[:, k, g * P : (g + 1) * P],
                        h1[k // H, k % H][:, lo : lo + wide],
                        start=(k == 0),
                        stop=False,
                    )
            for g in range(H):
                for k in range(early, T * H):
                    nc.tensor.matmul(
                        merged[g][:],
                        w2_sb[:, k, g * P : (g + 1) * P],
                        h1[k // H, k % H][:, lo : lo + wide],
                        start=False,
                        stop=(k == T * H - 1),
                    )
                h2[g, c] = held.tile([P, wide], BF16, name=f"h2_{g}_{c}")
                bias_relu(nc, turn, h2[g, c][:], merged[g][:], b2_sb[:, g : g + 1])
                turn += 1

        for c, (lo, wide) in enumerate(zip(STARTS, WIDTHS)):
            for e in range(H):
                dense = banks.tile([P, wide], F32, name="bank")
                for g in range(H):
                    nc.tensor.matmul(
                        dense[:],
                        wfc1_sb[:, g, e * P : (e + 1) * P],
                        h2[g, c][:],
                        start=(g == 0),
                        stop=(g == H - 1),
                    )
                result = held.tile([P, wide], F32, name=f"result_{e}_{c}", align_bytes=LINE)
                bias_relu(nc, turn, result[:], dense[:], bfc1_sb[:, e : e + 1])
                last = c == len(WIDTHS) - 1 and e == H - 1
                queue = nc.scalar if last else nc.sync
                queue.dma_start(out[e * P : (e + 1) * P, lo : lo + wide], result[:])
                turn += 1
